import numpy as np
import ml_dtypes


def mxq(x, axis, fmt="e4m3"):
    dtype, down = {"e4m3": (ml_dtypes.float8_e4m3fn, 7), "e5m2": (ml_dtypes.float8_e5m2, 14)}[fmt]
    v = np.moveaxis(np.asarray(x, np.float32).astype(ml_dtypes.bfloat16).astype(np.float64), axis, -1)
    blocks = v.reshape(v.shape[:-1] + (-1, 32))
    amax = np.abs(blocks).max(-1, keepdims=True)
    byte = np.maximum(np.where(amax > 0, np.frexp(amax)[1] - 1 + 127, 0) - down, 1)
    scale = np.exp2(byte - 127.0)
    codes = (blocks / scale).astype(np.float32).astype(dtype).astype(np.float64)
    return np.moveaxis((codes * scale).reshape(v.shape), -1, axis)


WIDE = False


def mx_kscale(k):
    if not WIDE:
        return np.ones(k)
    levels = np.array([10, -10, 5, -5, 0])
    a = np.random.permutation(np.resize(levels, k // 512 * 4)).reshape(k // 512, 4)
    idx = np.arange(k)
    return np.exp2(a[idx // 512, idx % 128 // 32])


BF16 = ml_dtypes.bfloat16


def bf(x):
    return np.asarray(x, np.float32).astype(BF16)


def f64(x):
    return np.asarray(x).astype(np.float64)


B, N, SR, SI, NH, NV, NC, NLON, NLAT = 2, 8, 1, 128, 4, 4, 32, 8, 8
S = SI * NH
MIN_SIGMA = 1e-10


def setup_inputs():
    s = mx_kscale(S)
    d = np.log2(s.max() / s)
    x0 = np.random.standard_normal((B, N, SR, S, NV, NC)) * 0.2 * np.sqrt(S)
    lon0 = np.random.standard_normal((B, N, SR, SI, NH))
    lat0 = np.random.standard_normal((B, N, SR, SI, NH))
    mus_lon = bf(np.linspace(-1.0, 1.0, NLON) + 0.03 * np.random.standard_normal(NLON))
    mus_lat = bf(np.linspace(-1.0, 1.0, NLAT) + 0.03 * np.random.standard_normal(NLAT))
    sigma = bf(0.4 + 0.2 * np.random.random(1))
    if d.max() > 0:
        sig = float(f64(sigma)[0])
        m0 = float(f64(mus_lon).min())
        lon0 = m0 - np.sqrt((0.3 * sig * lon0) ** 2 + 2.0 * np.log(2.0) * sig ** 2 * d.reshape(SI, NH))
    return {"x": bf(x0 * (2.0 ** d)[:, None, None]),
            "coords_lon": bf(lon0),
            "coords_lat": bf(lat0),
            "mus_lon": mus_lon,
            "mus_lat": mus_lat,
            "sigma": sigma}


def reference(x, coords_lon, coords_lat, mus_lon, mus_lat, sigma):
    x, coords_lon, coords_lat = f64(x), f64(coords_lon), f64(coords_lat)
    mus_lon, mus_lat, sigma = f64(mus_lon), f64(mus_lat), f64(sigma)
    b, n, sr, si, nh = coords_lon.shape
    nv, nc = x.shape[-2:]
    nlon, nlat = mus_lon.shape[0], mus_lat.shape[0]
    sig = np.maximum(sigma, MIN_SIGMA)
    wlon = np.exp(-0.5 * ((coords_lon[..., None] - mus_lon) / sig) ** 2)
    wlat = np.exp(-0.5 * ((coords_lat[..., None] - mus_lat) / sig) ** 2)
    w = (wlon[..., :, None] * wlat[..., None, :]).reshape(b, n, sr, si * nh, nlon, nlat)
    w = w / np.sum(w, axis=3, keepdims=True)
    wq = mxq(w, 3, "e4m3").reshape(b, n, sr, si * nh, nlon * nlat)
    xq = mxq(x, 3, "e4m3").reshape(b, n, sr, si * nh, nv * nc)
    out = xq.transpose(0, 1, 2, 4, 3) @ wq
    out = out.reshape(b, n, sr, nv, nc, nlon, nlat).transpose(0, 1, 2, 3, 5, 6, 4)
    return out.reshape(b, n * sr, nv, nlon, nlat, nc)

@@ -1,0 +1,224 @@
+from contextlib import ExitStack
+
+import concourse.mybir as mybir
+from concourse.masks import make_identity
+
+F32 = mybir.dt.float32
+BF16 = mybir.dt.bfloat16
+U32 = mybir.dt.uint32
+U8 = mybir.dt.uint8
+FP8X4 = mybir.dt.float8_e4m3fn_x4
+ACT = mybir.ActivationFunctionType
+ALU = mybir.AluOpType
+
+P = 128
+PACK = 4
+BATCH = 2
+PER_BATCH = 8
+OFFSETS = 8
+W_COLS = OFFSETS * OFFSETS
+X_COLS = 128
+C_LAST = 32
+PAIRS = 2
+CHUNKS = PER_BATCH // PAIRS
+UNITS = PAIRS * PACK
+BANK = 512
+SUMS = PAIRS * P
+LAG = 2
+MIN_SIGMA = 1e-10
+
+FLOPS = 2 * BATCH * PER_BATCH * P * PACK * X_COLS * W_COLS
+
+
+def tile_normal_nolayer_s_kernel(
+    tc, x, coords_lon, coords_lat, mus_lon, mus_lat, sigma, out
+):
+    nc = tc.nc
+    with ExitStack() as ctx:
+        keep = ctx.enter_context(tc.tile_pool(name="keep", bufs=1))
+        ps_coords = ctx.enter_context(tc.psum_pool(name="ps_coords", bufs=1))
+        ps_norm = ctx.enter_context(tc.psum_pool(name="ps_norm", bufs=CHUNKS))
+        ps_out = ctx.enter_context(tc.psum_pool(name="ps_out", bufs=3))
+        ctx.enter_context(tc.manual_schedule())
+
+        coords = keep.tile([P, P], BF16)
+        mus = keep.tile([P, 2, 16], BF16)
+        sigma_bf = keep.tile([P, 1], BF16)
+        x_rows = keep.tile([P, CHUNKS, BATCH, PAIRS, PACK, X_COLS], BF16)
+        ident_bf = keep.tile([P, P], BF16)
+        ident_f32 = keep.tile([P, P], F32)
+        ones = keep.tile([P, 1], F32)
+        table_warm = keep.tile([P, 1], F32)
+        sigma_f32 = keep.tile([P, 1], F32)
+        inv_sigma = keep.tile([P, 1], F32)
+        gauss = keep.tile([P, CHUNKS, 2, UNITS * BATCH, OFFSETS], F32)
+        g = keep.tile([P, CHUNKS, UNITS, BATCH * W_COLS], F32)
+        inv_sums = keep.tile([P, CHUNKS, PAIRS], F32)
+        x_grouped = keep.tile([P, CHUNKS, PAIRS, BATCH, X_COLS, PACK], BF16, align_bytes=64)
+        x_codes = keep.tile([P, CHUNKS, PAIRS * BATCH * X_COLS], U32, align_bytes=64)
+        x_scales = keep.tile([P, CHUNKS, PAIRS * BATCH * X_COLS], U8, align_bytes=64)
+        w_bf = keep.tile([P, CHUNKS, PAIRS, P, PACK], BF16, align_bytes=64)
+        w_codes = keep.tile([P, CHUNKS, PAIRS * P], U32, align_bytes=64)
+        w_scales = keep.tile([P, CHUNKS, PAIRS * P], U8, align_bytes=64)
+        result = keep.tile([P, CHUNKS, PAIRS, X_COLS], F32)
+        coords_t = ps_coords.tile([P, P], BF16)
+        norms = [ps_norm.tile([P, BANK], F32, name="norm") for c in range(CHUNKS)]
+
+        for w, coords_w in enumerate((coords_lon, coords_lat)):
+            for a in range(BATCH):
+                nc.sync.dma_start(
+                    out=coords[w * 64 + a : (w + 1) * 64 : BATCH, :],
+                    in_=coords_w[a].rearrange("j o (t i) h -> (j o t) (i h)", t=PACK),
+                )
+        nc.scalar.dma_start(out=mus[:, 0, 0:OFFSETS], in_=mus_lon.partition_broadcast(P))
+        nc.scalar.dma_start(out=mus[:, 1, 0:OFFSETS], in_=mus_lat.partition_broadcast(P))
+        nc.scalar.dma_start(out=sigma_bf[:], in_=sigma.partition_broadcast(P))
+        for c in range(CHUNKS):
+            for a in range(BATCH):
+                nc.sync.dma_start(
+                    out=x_rows[:, c, a].rearrange("p j t n -> p (j t) n"),
+                    in_=x[a, c * PAIRS : (c + 1) * PAIRS, 0].rearrange(
+                        "j (t p) v k -> p (j t) (v k)", p=P
+                    ),
+                )
+
+        make_identity(nc, ident_bf[:])
+        make_identity(nc, ident_f32[:])
+        nc.vector.memset(ones[:], 1.0)
+        nc.scalar.activation(out=table_warm[:], in_=ones[:], func=ACT.Exp)
+        nc.vector.tensor_scalar_max(out=sigma_f32[:], in0=sigma_bf[:], scalar1=MIN_SIGMA)
+        nc.vector.reciprocal(out=inv_sigma[:], in_=sigma_f32[:])
+
+        nc.tensor.transpose(out=coords_t[:], in_=coords[:], identity=ident_bf[:])
+        coords_by_chunk = coords_t[:].rearrange("p (w c e) -> p c w e", w=2, c=CHUNKS)
+
+        def gaussians(c):
+            shape = [P, 2, UNITS * BATCH, OFFSETS]
+            nc.vector.tensor_tensor(
+                out=gauss[:, c],
+                in0=coords_by_chunk[:, c].unsqueeze(3).to_broadcast(shape),
+                in1=mus[:, :, 0:OFFSETS].unsqueeze(2).to_broadcast(shape),
+                op=ALU.subtract,
+            )
+            flat = gauss[:, c].rearrange("p w e m -> p (w e m)")
+            nc.scalar.activation(out=flat, in_=flat, func=ACT.Square, scale=inv_sigma[:, 0:1])
+            nc.scalar.activation(out=flat, in_=flat, func=ACT.Exp, scale=-0.5)
+
+        def products(c):
+            shape = [P, UNITS * BATCH, OFFSETS, OFFSETS]
+            nc.vector.tensor_tensor(
+                out=g[:, c].rearrange("p u (a m n) -> p (u a) m n", a=BATCH, m=OFFSETS),
+                in0=gauss[:, c, 0].unsqueeze(3).to_broadcast(shape),
+                in1=gauss[:, c, 1].unsqueeze(2).to_broadcast(shape),
+                op=ALU.mult,
+            )
+
+        def sums(c):
+            for j in range(PAIRS):
+                for t in range(PACK):
+                    nc.tensor.matmul(
+                        out=norms[c][:, SUMS + j : SUMS + j + 1],
+                        lhsT=g[:, c, j * PACK + t],
+                        rhs=ones[:, 0:1],
+                        start=(t == 0),
+                        stop=(t == PACK - 1),
+                    )
+
+        def invert(c):
+            nc.vector.reciprocal(out=inv_sums[:, c], in_=norms[c][:, SUMS : SUMS + PAIRS])
+
+        def spread(c):
+            for j in range(PAIRS):
+                nc.tensor.transpose(
+                    out=norms[c][:, j * P : (j + 1) * P],
+                    in_=inv_sums[:, c, j : j + 1].to_broadcast([P, P]),
+                    identity=ident_f32[:],
+                )
+
+        def regroup_x(c):
+            for j in range(PAIRS):
+                for a in range(BATCH):
+                    nc.scalar.copy(
+                        out=x_grouped[:, c, j, a].rearrange("p (n i) t -> p n t i", i=4),
+                        in_=x_rows[:, c, a, j].rearrange("p t (n i) -> p n t i", i=4),
+                    )
+
+        def quantise_x(c):
+            nc.vector.quantize_mx(
+                out=x_codes[:, c].bitcast(FP8X4),
+                scales=x_scales[:, c],
+                in_=x_grouped[:, c].rearrange("p j a n t -> p (j a n t)"),
+            )
+
+        def normalise(c):
+            shape = [P, PAIRS, P, PACK]
+            nc.vector.tensor_tensor(
+                out=w_bf[:, c],
+                in0=g[:, c].rearrange("p (j t) n -> p j n t", t=PACK),
+                in1=norms[c][:, 0:SUMS]
+                .rearrange("p (j n) -> p j n", j=PAIRS)
+                .unsqueeze(3)
+                .to_broadcast(shape),
+                op=ALU.mult,
+            )
+
+        def quantise_w(c):
+            nc.vector.quantize_mx(
+                out=w_codes[:, c].bitcast(FP8X4),
+                scales=w_scales[:, c],
+                in_=w_bf[:, c].rearrange("p j n t -> p (j n t)"),
+            )
+
+        accs = {}
+
+        def multiply(c):
+            accs[c] = ps_out.tile([P, PAIRS, BATCH, X_COLS], F32, name="acc")
+            for j in range(PAIRS):
+                w_cols = slice(j * P, (j + 1) * P)
+                x_cols = slice(j * BATCH * X_COLS, (j + 1) * BATCH * X_COLS)
+                nc.tensor.matmul_mx(
+                    out=accs[c][:, j].rearrange("p a n -> p (a n)"),
+                    lhsT=w_codes[:, c, w_cols].bitcast(FP8X4),
+                    lhsT_scale=w_scales[:, c, w_cols],
+                    rhs=x_codes[:, c, x_cols].bitcast(FP8X4),
+                    rhs_scale=x_scales[:, c, x_cols],
+                    start=True,
+                    stop=True,
+                )
+
+        def store(c):
+            nc.vector.tensor_copy(out=result[0:64, c], in_=accs[c][0:64, :, 0, :])
+            nc.scalar.copy(out=result[64:128, c], in_=accs[c][64:128, :, 1, :])
+            for a in range(BATCH):
+                nc.sync.dma_start(
+                    out=out[a, c * PAIRS : (c + 1) * PAIRS].rearrange(
+                        "j v m n k -> (m n) (j v) k"
+                    ),
+                    in_=result[a * 64 : (a + 1) * 64, c].rearrange(
+                        "p j (v k) -> p (j v) k", k=C_LAST
+                    ),
+                )
+
+        for c in range(CHUNKS):
+            gaussians(c)
+        for c in range(CHUNKS):
+            regroup_x(c)
+        for c in range(CHUNKS):
+            products(c)
+            if c >= LAG:
+                invert(c - LAG)
+                spread(c - LAG)
+            sums(c)
+        quantise_x(0)
+        for c in range(CHUNKS):
+            normalise(c)
+            if c < LAG:
+                invert(c + CHUNKS - LAG)
+                spread(c + CHUNKS - LAG)
+            if c >= 1:
+                store(c - 1)
+            quantise_w(c)
+            if c + 1 < CHUNKS:
+                quantise_x(c + 1)
+            multiply(c)
+        store(CHUNKS - 1)

@@ -23,7 +23,7 @@ PAIRS = 2
 CHUNKS = PER_BATCH // PAIRS
 UNITS = PAIRS * PACK
 BANK = 512
-SUMS = PAIRS * P
+SPREAD = PAIRS * P
 LAG = 2
 MIN_SIGMA = 1e-10
 
@@ -53,6 +53,7 @@ def tile_normal_nolayer_s_kernel(
         inv_sigma = keep.tile([P, 1], F32)
         gauss = keep.tile([P, CHUNKS, 2, UNITS * BATCH, OFFSETS], F32)
         g = keep.tile([P, CHUNKS, UNITS, BATCH * W_COLS], F32)
+        g_sums = keep.tile([P, CHUNKS, PAIRS], F32)
         inv_sums = keep.tile([P, CHUNKS, PAIRS], F32)
         x_grouped = keep.tile([P, CHUNKS, PAIRS, BATCH, X_COLS, PACK], BF16, align_bytes=64)
         x_codes = keep.tile([P, CHUNKS, PAIRS * BATCH * X_COLS], U32, align_bytes=64)
@@ -117,20 +118,27 @@ def tile_normal_nolayer_s_kernel(
             for j in range(PAIRS):
                 for t in range(PACK):
                     nc.tensor.matmul(
-                        out=norms[c][:, SUMS + j : SUMS + j + 1],
+                        out=norms[c][:, j * P : (j + 1) * P],
                         lhsT=g[:, c, j * PACK + t],
-                        rhs=ones[:, 0:1],
+                        rhs=ident_f32[:],
+                        is_transpose=True,
                         start=(t == 0),
                         stop=(t == PACK - 1),
                     )
 
         def invert(c):
-            nc.vector.reciprocal(out=inv_sums[:, c], in_=norms[c][:, SUMS : SUMS + PAIRS])
+            nc.vector.tensor_reduce(
+                out=g_sums[:, c],
+                in_=norms[c][:, 0:SPREAD].rearrange("p (j i) -> p j i", j=PAIRS),
+                axis=mybir.AxisListType.X,
+                op=ALU.add,
+            )
+            nc.vector.reciprocal(out=inv_sums[:, c], in_=g_sums[:, c])
 
         def spread(c):
             for j in range(PAIRS):
                 nc.tensor.transpose(
-                    out=norms[c][:, j * P : (j + 1) * P],
+                    out=norms[c][:, SPREAD + j * P : SPREAD + (j + 1) * P],
                     in_=inv_sums[:, c, j : j + 1].to_broadcast([P, P]),
                     identity=ident_f32[:],
                 )
@@ -155,7 +163,7 @@ def tile_normal_nolayer_s_kernel(
             nc.vector.tensor_tensor(
                 out=w_bf[:, c],
                 in0=g[:, c].rearrange("p (j t) n -> p j n t", t=PACK),
-                in1=norms[c][:, 0:SUMS]
+                in1=norms[c][:, SPREAD : SPREAD + PAIRS * P]
                 .rearrange("p (j n) -> p j n", j=PAIRS)
                 .unsqueeze(3)
                 .to_broadcast(shape),

@@ -24,7 +24,7 @@ CHUNKS = PER_BATCH // PAIRS
 UNITS = PAIRS * PACK
 BANK = 512
 SPREAD = PAIRS * P
-LAG = 2
+POOL_CHUNKS = 2
 MIN_SIGMA = 1e-10
 
 FLOPS = 2 * BATCH * PER_BATCH * P * PACK * X_COLS * W_COLS
@@ -107,7 +107,8 @@ def tile_normal_nolayer_s_kernel(
 
         def products(c):
             shape = [P, UNITS * BATCH, OFFSETS, OFFSETS]
-            nc.vector.tensor_tensor(
+            engine = nc.vector if c < CHUNKS - POOL_CHUNKS else nc.gpsimd
+            engine.tensor_tensor(
                 out=g[:, c].rearrange("p u (a m n) -> p (u a) m n", a=BATCH, m=OFFSETS),
                 in0=gauss[:, c, 0].unsqueeze(3).to_broadcast(shape),
                 in1=gauss[:, c, 1].unsqueeze(2).to_broadcast(shape),
@@ -194,8 +195,8 @@ def tile_normal_nolayer_s_kernel(
                     stop=True,
                 )
 
-        def store(c):
-            nc.vector.tensor_copy(out=result[0:64, c], in_=accs[c][0:64, :, 0, :])
+        def store(c, first_half):
+            first_half(out=result[0:64, c], in_=accs[c][0:64, :, 0, :])
             nc.scalar.copy(out=result[64:128, c], in_=accs[c][64:128, :, 1, :])
             for a in range(BATCH):
                 nc.sync.dma_start(
@@ -213,20 +214,20 @@ def tile_normal_nolayer_s_kernel(
             regroup_x(c)
         for c in range(CHUNKS):
             products(c)
-            if c >= LAG:
-                invert(c - LAG)
-                spread(c - LAG)
-            sums(c)
-        quantise_x(0)
+        sums(0)
+        invert(0)
+        spread(0)
+        sums(1)
         for c in range(CHUNKS):
             normalise(c)
-            if c < LAG:
-                invert(c + CHUNKS - LAG)
-                spread(c + CHUNKS - LAG)
-            if c >= 1:
-                store(c - 1)
-            quantise_w(c)
             if c + 1 < CHUNKS:
-                quantise_x(c + 1)
+                invert(c + 1)
+                spread(c + 1)
+            if c + 2 < CHUNKS:
+                sums(c + 2)
+            quantise_x(c)
+            quantise_w(c)
             multiply(c)
-        store(CHUNKS - 1)
+            if c >= 1:
+                store(c - 1, nc.scalar.copy)
+        store(CHUNKS - 1, nc.vector.tensor_copy)

@@ -41,17 +41,17 @@ def tile_normal_nolayer_s_kernel(
         ps_out = ctx.enter_context(tc.psum_pool(name="ps_out", bufs=3))
         ctx.enter_context(tc.manual_schedule())
 
-        coords = keep.tile([P, P], BF16)
+        coords = keep.tile([P, 2 * P], BF16)
         mus = keep.tile([P, 2, 16], BF16)
+        mus_by_group = keep.tile([P, 2 * BATCH, OFFSETS], F32)
         sigma_bf = keep.tile([P, 1], BF16)
         x_rows = keep.tile([P, CHUNKS, BATCH, PAIRS, PACK, X_COLS], BF16)
-        ident_bf = keep.tile([P, P], BF16)
         ident_f32 = keep.tile([P, P], F32)
         ones = keep.tile([P, 1], F32)
         table_warm = keep.tile([P, 1], F32)
         sigma_f32 = keep.tile([P, 1], F32)
         inv_sigma = keep.tile([P, 1], F32)
-        gauss = keep.tile([P, CHUNKS, 2, UNITS * BATCH, OFFSETS], F32)
+        gauss = keep.tile([P, CHUNKS, 2 * BATCH, UNITS, OFFSETS], F32)
         g = keep.tile([P, CHUNKS, UNITS, BATCH * W_COLS], F32)
         g_sums = keep.tile([P, CHUNKS, PAIRS], F32)
         inv_sums = keep.tile([P, CHUNKS, PAIRS], F32)
@@ -62,58 +62,69 @@ def tile_normal_nolayer_s_kernel(
         w_codes = keep.tile([P, CHUNKS, PAIRS * P], U32, align_bytes=64)
         w_scales = keep.tile([P, CHUNKS, PAIRS * P], U8, align_bytes=64)
         result = keep.tile([P, CHUNKS, PAIRS, X_COLS], F32)
-        coords_t = ps_coords.tile([P, P], BF16)
+        coords_t = ps_coords.tile([P, P], F32)
         norms = [ps_norm.tile([P, BANK], F32, name="norm") for c in range(CHUNKS)]
 
+        nc.vector.memset(coords[64:128, :], 0.0)
         for w, coords_w in enumerate((coords_lon, coords_lat)):
-            for a in range(BATCH):
-                nc.sync.dma_start(
-                    out=coords[w * 64 + a : (w + 1) * 64 : BATCH, :],
-                    in_=coords_w[a].rearrange("j o (t i) h -> (j o t) (i h)", t=PACK),
-                )
+            nc.sync.dma_start(
+                out=coords[w * 32 : (w + 1) * 32, :],
+                in_=coords_w.rearrange("a j o (u i) h -> (a j o u) (i h)", u=2),
+            )
         nc.scalar.dma_start(out=mus[:, 0, 0:OFFSETS], in_=mus_lon.partition_broadcast(P))
         nc.scalar.dma_start(out=mus[:, 1, 0:OFFSETS], in_=mus_lat.partition_broadcast(P))
         nc.scalar.dma_start(out=sigma_bf[:], in_=sigma.partition_broadcast(P))
         for c in range(CHUNKS):
             for a in range(BATCH):
                 nc.sync.dma_start(
-                    out=x_rows[:, c, a].rearrange("p j t n -> p (j t) n"),
+                    out=x_rows[:, c, a].rearrange("p j (u e) n -> p (j u) (e n)", u=2),
                     in_=x[a, c * PAIRS : (c + 1) * PAIRS, 0].rearrange(
-                        "j (t p) v k -> p (j t) (v k)", p=P
+                        "j (u p e) v k -> p (j u) (e v k)", u=2, e=2
                     ),
                 )
 
-        make_identity(nc, ident_bf[:])
         make_identity(nc, ident_f32[:])
         nc.vector.memset(ones[:], 1.0)
         nc.scalar.activation(out=table_warm[:], in_=ones[:], func=ACT.Exp)
         nc.vector.tensor_scalar_max(out=sigma_f32[:], in0=sigma_bf[:], scalar1=MIN_SIGMA)
         nc.vector.reciprocal(out=inv_sigma[:], in_=sigma_f32[:])
 
-        nc.tensor.transpose(out=coords_t[:], in_=coords[:], identity=ident_bf[:])
-        coords_by_chunk = coords_t[:].rearrange("p (w c e) -> p c w e", w=2, c=CHUNKS)
+        nc.vector.tensor_copy(
+            out=mus_by_group[:].rearrange("p (w a) m -> p w a m", a=BATCH),
+            in_=mus[:, :, 0:OFFSETS].unsqueeze(2).to_broadcast([P, 2, BATCH, OFFSETS]),
+        )
+
+        nc.tensor.transpose(
+            out=coords_t[:], in_=coords[:].bitcast(F32), identity=ident_f32[:]
+        )
+        coords_by_chunk = coords_t[:].bitcast(BF16)[:, 0:P].rearrange(
+            "p (g c u) -> p c g u", g=2 * BATCH, c=CHUNKS
+        )
 
         def gaussians(c):
-            shape = [P, 2, UNITS * BATCH, OFFSETS]
+            shape = [P, 2 * BATCH, UNITS, OFFSETS]
             nc.vector.tensor_tensor(
                 out=gauss[:, c],
                 in0=coords_by_chunk[:, c].unsqueeze(3).to_broadcast(shape),
-                in1=mus[:, :, 0:OFFSETS].unsqueeze(2).to_broadcast(shape),
+                in1=mus_by_group[:].unsqueeze(2).to_broadcast(shape),
                 op=ALU.subtract,
             )
-            flat = gauss[:, c].rearrange("p w e m -> p (w e m)")
+            flat = gauss[:, c].rearrange("p g u m -> p (g u m)")
             nc.scalar.activation(out=flat, in_=flat, func=ACT.Square, scale=inv_sigma[:, 0:1])
             nc.scalar.activation(out=flat, in_=flat, func=ACT.Exp, scale=-0.5)
 
         def products(c):
-            shape = [P, UNITS * BATCH, OFFSETS, OFFSETS]
+            shape = [P, UNITS, OFFSETS, OFFSETS]
             engine = nc.vector if c < CHUNKS - POOL_CHUNKS else nc.gpsimd
-            engine.tensor_tensor(
-                out=g[:, c].rearrange("p u (a m n) -> p (u a) m n", a=BATCH, m=OFFSETS),
-                in0=gauss[:, c, 0].unsqueeze(3).to_broadcast(shape),
-                in1=gauss[:, c, 1].unsqueeze(2).to_broadcast(shape),
-                op=ALU.mult,
-            )
+            for a in range(BATCH):
+                engine.tensor_tensor(
+                    out=g[:, c, :, a * W_COLS : (a + 1) * W_COLS].rearrange(
+                        "p u (m n) -> p u m n", m=OFFSETS
+                    ),
+                    in0=gauss[:, c, a].unsqueeze(3).to_broadcast(shape),
+                    in1=gauss[:, c, BATCH + a].unsqueeze(2).to_broadcast(shape),
+                    op=ALU.mult,
+                )
 
         def sums(c):
             for j in range(PAIRS):
@@ -145,8 +156,8 @@ def tile_normal_nolayer_s_kernel(
                 )
 
         def regroup_x(c):
-            for j in range(PAIRS):
-                for a in range(BATCH):
+            for a in range(BATCH):
+                for j in range(PAIRS):
                     nc.scalar.copy(
                         out=x_grouped[:, c, j, a].rearrange("p (n i) t -> p n t i", i=4),
                         in_=x_rows[:, c, a, j].rearrange("p t (n i) -> p n t i", i=4),

from contextlib import ExitStack

import concourse.mybir as mybir
from concourse.masks import make_identity

F32 = mybir.dt.float32
BF16 = mybir.dt.bfloat16
U32 = mybir.dt.uint32
U8 = mybir.dt.uint8
FP8X4 = mybir.dt.float8_e4m3fn_x4
ACT = mybir.ActivationFunctionType
ALU = mybir.AluOpType

P = 128
PACK = 4
BATCH = 2
PER_BATCH = 8
OFFSETS = 8
W_COLS = OFFSETS * OFFSETS
X_COLS = 128
C_LAST = 32
PAIRS = 2
CHUNKS = PER_BATCH // PAIRS
UNITS = PAIRS * PACK
BANK = 512
SPREAD = PAIRS * P
POOL_CHUNKS = 2
MIN_SIGMA = 1e-10

FLOPS = 2 * BATCH * PER_BATCH * P * PACK * X_COLS * W_COLS


def tile_normal_nolayer_s_kernel(
    tc, x, coords_lon, coords_lat, mus_lon, mus_lat, sigma, out
):
    nc = tc.nc
    with ExitStack() as ctx:
        keep = ctx.enter_context(tc.tile_pool(name="keep", bufs=1))
        ps_coords = ctx.enter_context(tc.psum_pool(name="ps_coords", bufs=1))
        ps_norm = ctx.enter_context(tc.psum_pool(name="ps_norm", bufs=CHUNKS))
        ps_out = ctx.enter_context(tc.psum_pool(name="ps_out", bufs=3))
        ctx.enter_context(tc.manual_schedule())

        coords = keep.tile([P, 2 * P], BF16)
        mus = keep.tile([P, 2, 16], BF16)
        mus_by_group = keep.tile([P, 2 * BATCH, OFFSETS], F32)
        sigma_bf = keep.tile([P, 1], BF16)
        x_rows = keep.tile([P, CHUNKS, BATCH, PAIRS, PACK, X_COLS], BF16)
        ident_f32 = keep.tile([P, P], F32)
        ones = keep.tile([P, 1], F32)
        table_warm = keep.tile([P, 1], F32)
        sigma_f32 = keep.tile([P, 1], F32)
        inv_sigma = keep.tile([P, 1], F32)
        gauss = keep.tile([P, CHUNKS, 2 * BATCH, UNITS, OFFSETS], F32)
        g = keep.tile([P, CHUNKS, UNITS, BATCH * W_COLS], F32)
        g_sums = keep.tile([P, CHUNKS, PAIRS], F32)
        inv_sums = keep.tile([P, CHUNKS, PAIRS], F32)
        x_grouped = keep.tile([P, CHUNKS, PAIRS, BATCH, X_COLS, PACK], BF16, align_bytes=64)
        x_codes = keep.tile([P, CHUNKS, PAIRS * BATCH * X_COLS], U32, align_bytes=64)
        x_scales = keep.tile([P, CHUNKS, PAIRS * BATCH * X_COLS], U8, align_bytes=64)
        w_bf = keep.tile([P, CHUNKS, PAIRS, P, PACK], BF16, align_bytes=64)
        w_codes = keep.tile([P, CHUNKS, PAIRS * P], U32, align_bytes=64)
        w_scales = keep.tile([P, CHUNKS, PAIRS * P], U8, align_bytes=64)
        result = keep.tile([P, CHUNKS, PAIRS, X_COLS], F32)
        coords_t = ps_coords.tile([P, P], F32)
        norms = [ps_norm.tile([P, BANK], F32, name="norm") for c in range(CHUNKS)]

        nc.vector.memset(coords[64:128, :], 0.0)
        for w, coords_w in enumerate((coords_lon, coords_lat)):
            nc.sync.dma_start(
                out=coords[w * 32 : (w + 1) * 32, :],
                in_=coords_w.rearrange("a j o (u i) h -> (a j o u) (i h)", u=2),
            )
        nc.scalar.dma_start(out=mus[:, 0, 0:OFFSETS], in_=mus_lon.partition_broadcast(P))
        nc.scalar.dma_start(out=mus[:, 1, 0:OFFSETS], in_=mus_lat.partition_broadcast(P))
        nc.scalar.dma_start(out=sigma_bf[:], in_=sigma.partition_broadcast(P))
        for c in range(CHUNKS):
            for a in range(BATCH):
                nc.sync.dma_start(
                    out=x_rows[:, c, a].rearrange("p j (u e) n -> p (j u) (e n)", u=2),
                    in_=x[a, c * PAIRS : (c + 1) * PAIRS, 0].rearrange(
                        "j (u p e) v k -> p (j u) (e v k)", u=2, e=2
                    ),
                )

        make_identity(nc, ident_f32[:])
        nc.vector.memset(ones[:], 1.0)
        nc.scalar.activation(out=table_warm[:], in_=ones[:], func=ACT.Exp)
        nc.vector.tensor_scalar_max(out=sigma_f32[:], in0=sigma_bf[:], scalar1=MIN_SIGMA)
        nc.vector.reciprocal(out=inv_sigma[:], in_=sigma_f32[:])

        nc.vector.tensor_copy(
            out=mus_by_group[:].rearrange("p (w a) m -> p w a m", a=BATCH),
            in_=mus[:, :, 0:OFFSETS].unsqueeze(2).to_broadcast([P, 2, BATCH, OFFSETS]),
        )

        nc.tensor.transpose(
            out=coords_t[:], in_=coords[:].bitcast(F32), identity=ident_f32[:]
        )
        coords_by_chunk = coords_t[:].bitcast(BF16)[:, 0:P].rearrange(
            "p (g c u) -> p c g u", g=2 * BATCH, c=CHUNKS
        )

        def gaussians(c):
            shape = [P, 2 * BATCH, UNITS, OFFSETS]
            nc.vector.tensor_tensor(
                out=gauss[:, c],
                in0=coords_by_chunk[:, c].unsqueeze(3).to_broadcast(shape),
                in1=mus_by_group[:].unsqueeze(2).to_broadcast(shape),
                op=ALU.subtract,
            )
            flat = gauss[:, c].rearrange("p g u m -> p (g u m)")
            nc.scalar.activation(out=flat, in_=flat, func=ACT.Square, scale=inv_sigma[:, 0:1])
            nc.scalar.activation(out=flat, in_=flat, func=ACT.Exp, scale=-0.5)

        def products(c):
            shape = [P, UNITS, OFFSETS, OFFSETS]
            engine = nc.vector if c < CHUNKS - POOL_CHUNKS else nc.gpsimd
            for a in range(BATCH):
                engine.tensor_tensor(
                    out=g[:, c, :, a * W_COLS : (a + 1) * W_COLS].rearrange(
                        "p u (m n) -> p u m n", m=OFFSETS
                    ),
                    in0=gauss[:, c, a].unsqueeze(3).to_broadcast(shape),
                    in1=gauss[:, c, BATCH + a].unsqueeze(2).to_broadcast(shape),
                    op=ALU.mult,
                )

        def sums(c):
            for j in range(PAIRS):
                for t in range(PACK):
                    nc.tensor.matmul(
                        out=norms[c][:, j * P : (j + 1) * P],
                        lhsT=g[:, c, j * PACK + t],
                        rhs=ident_f32[:],
                        is_transpose=True,
                        start=(t == 0),
                        stop=(t == PACK - 1),
                    )

        def invert(c):
            nc.vector.tensor_reduce(
                out=g_sums[:, c],
                in_=norms[c][:, 0:SPREAD].rearrange("p (j i) -> p j i", j=PAIRS),
                axis=mybir.AxisListType.X,
                op=ALU.add,
            )
            nc.vector.reciprocal(out=inv_sums[:, c], in_=g_sums[:, c])

        def spread(c):
            for j in range(PAIRS):
                nc.tensor.transpose(
                    out=norms[c][:, SPREAD + j * P : SPREAD + (j + 1) * P],
                    in_=inv_sums[:, c, j : j + 1].to_broadcast([P, P]),
                    identity=ident_f32[:],
                )

        def regroup_x(c):
            for a in range(BATCH):
                for j in range(PAIRS):
                    nc.scalar.copy(
                        out=x_grouped[:, c, j, a].rearrange("p (n i) t -> p n t i", i=4),
                        in_=x_rows[:, c, a, j].rearrange("p t (n i) -> p n t i", i=4),
                    )

        def quantise_x(c):
            nc.vector.quantize_mx(
                out=x_codes[:, c].bitcast(FP8X4),
                scales=x_scales[:, c],
                in_=x_grouped[:, c].rearrange("p j a n t -> p (j a n t)"),
            )

        def normalise(c):
            shape = [P, PAIRS, P, PACK]
            nc.vector.tensor_tensor(
                out=w_bf[:, c],
                in0=g[:, c].rearrange("p (j t) n -> p j n t", t=PACK),
                in1=norms[c][:, SPREAD : SPREAD + PAIRS * P]
                .rearrange("p (j n) -> p j n", j=PAIRS)
                .unsqueeze(3)
                .to_broadcast(shape),
                op=ALU.mult,
            )

        def quantise_w(c):
            nc.vector.quantize_mx(
                out=w_codes[:, c].bitcast(FP8X4),
                scales=w_scales[:, c],
                in_=w_bf[:, c].rearrange("p j n t -> p (j n t)"),
            )

        accs = {}

        def multiply(c):
            accs[c] = ps_out.tile([P, PAIRS, BATCH, X_COLS], F32, name="acc")
            for j in range(PAIRS):
                w_cols = slice(j * P, (j + 1) * P)
                x_cols = slice(j * BATCH * X_COLS, (j + 1) * BATCH * X_COLS)
                nc.tensor.matmul_mx(
                    out=accs[c][:, j].rearrange("p a n -> p (a n)"),
                    lhsT=w_codes[:, c, w_cols].bitcast(FP8X4),
                    lhsT_scale=w_scales[:, c, w_cols],
                    rhs=x_codes[:, c, x_cols].bitcast(FP8X4),
                    rhs_scale=x_scales[:, c, x_cols],
                    start=True,
                    stop=True,
                )

        def store(c, first_half):
            first_half(out=result[0:64, c], in_=accs[c][0:64, :, 0, :])
            nc.scalar.copy(out=result[64:128, c], in_=accs[c][64:128, :, 1, :])
            for a in range(BATCH):
                nc.sync.dma_start(
                    out=out[a, c * PAIRS : (c + 1) * PAIRS].rearrange(
                        "j v m n k -> (m n) (j v) k"
                    ),
                    in_=result[a * 64 : (a + 1) * 64, c].rearrange(
                        "p j (v k) -> p (j v) k", k=C_LAST
                    ),
                )

        for c in range(CHUNKS):
            gaussians(c)
        for c in range(CHUNKS):
            regroup_x(c)
        for c in range(CHUNKS):
            products(c)
        sums(0)
        invert(0)
        spread(0)
        sums(1)
        for c in range(CHUNKS):
            normalise(c)
            if c + 1 < CHUNKS:
                invert(c + 1)
                spread(c + 1)
            if c + 2 < CHUNKS:
                sums(c + 2)
            quantise_x(c)
            quantise_w(c)
            multiply(c)
            if c >= 1:
                store(c - 1, nc.scalar.copy)
        store(CHUNKS - 1, nc.vector.tensor_copy)
